import numpy as np
import ml_dtypes


def mxq(x, axis, fmt="e4m3"):
    dtype, down = {"e4m3": (ml_dtypes.float8_e4m3fn, 7), "e5m2": (ml_dtypes.float8_e5m2, 14)}[fmt]
    v = np.moveaxis(np.asarray(x, np.float32).astype(ml_dtypes.bfloat16).astype(np.float64), axis, -1)
    blocks = v.reshape(v.shape[:-1] + (-1, 32))
    amax = np.abs(blocks).max(-1, keepdims=True)
    byte = np.maximum(np.where(amax > 0, np.frexp(amax)[1] - 1 + 127, 0) - down, 1)
    scale = np.exp2(byte - 127.0)
    codes = (blocks / scale).astype(np.float32).astype(dtype).astype(np.float64)
    return np.moveaxis((codes * scale).reshape(v.shape), -1, axis)


WIDE = False


def mx_kscale(k):
    if not WIDE:
        return np.ones(k)
    levels = np.array([20, -20, 10, -10, 0])
    a = np.random.permutation(np.resize(levels, k // 512 * 4)).reshape(k // 512, 4)
    idx = np.arange(k)
    return np.exp2(a[idx // 512, idx % 128 // 32])


BF16 = ml_dtypes.bfloat16


def bf(x):
    return np.asarray(x, np.float32).astype(BF16)


def f64(x):
    return np.asarray(x).astype(np.float64)


B, S, D, E, R = 2, 1024, 4096, 8, 64
T = B * S


def setup_inputs():
    s = mx_kscale(T).reshape(B, S)
    x = np.random.standard_normal((B, S, D)) * s[:, :, None]
    W = np.random.standard_normal((E, R, D)) * (1.0 / np.sqrt(D))
    g = (np.random.standard_normal((E, B, S, R))
         * np.exp2(np.random.randint(-12, 1, (1, B, S, 1))) / s[None, :, :, None])
    return {"x": bf(x), "W": bf(W), "grad_out": bf(g)}


def reference(x, W, grad_out):
    xt = f64(x).reshape(T, D)
    gt = f64(grad_out).transpose(1, 2, 0, 3).reshape(T, E * R)
    gw = mxq(gt, 0, "e5m2").T @ mxq(xt, 0, "e4m3")
    return gw.reshape(E, R, D)

@@ -1,0 +1,194 @@
+from contextlib import ExitStack
+
+import concourse.mybir as mybir
+
+BF16 = mybir.dt.bfloat16
+F32 = mybir.dt.float32
+U32 = mybir.dt.uint32
+U8 = mybir.dt.uint8
+E4M3X4 = mybir.dt.float8_e4m3fn_x4
+E5M2X4 = mybir.dt.float8_e5m2_x4
+
+P = 128
+PACK = 4
+K_PASS = P * PACK
+TOKENS = 2048
+D = 4096
+EXPERTS = 8
+RANK = 64
+M_ALL = EXPERTS * RANK
+PASSES = TOKENS // K_PASS
+M_TILES = M_ALL // P
+N_TILE = 512
+CHUNK = 1024
+N_PER_CHUNK = CHUNK // N_TILE
+ROUNDS = D // CHUNK
+CHUNKS = ROUNDS * PASSES
+
+FLOPS = 2 * TOKENS * M_ALL * D
+BYTES = TOKENS * D * 2 + TOKENS * M_ALL * 2 + M_ALL * D * 4
+
+RAW_BUFS = 10
+STAGE_BUFS = 12
+CODE_BUFS = 6
+GROUPED_BUFS = 3
+V_COLS = 672
+V_EXPERTS = 2
+TAIL_PAIRS = 4
+
+
+def tile_moelineara_kernel(tc, x, W, grad_out, out):
+    nc = tc.nc
+    x_rows = x.rearrange("b s d -> (b s) d")
+    g_rows = grad_out.rearrange("e b s r -> e (b s) r")
+    out_rows = out.rearrange("e r d -> (e r) d")
+
+    with ExitStack() as ctx:
+        ctx.enter_context(tc.manual_schedule())
+        raw_pool = ctx.enter_context(tc.tile_pool(name="raw", bufs=RAW_BUFS))
+        graw_pool = ctx.enter_context(tc.tile_pool(name="graw", bufs=PASSES))
+        grouped_pool = ctx.enter_context(tc.tile_pool(name="grouped", bufs=GROUPED_BUFS))
+        ggrouped_pool = ctx.enter_context(tc.tile_pool(name="ggrouped", bufs=2))
+        code_pool = ctx.enter_context(tc.tile_pool(name="codes", bufs=CODE_BUFS))
+        keep_pool = ctx.enter_context(tc.tile_pool(name="keep", bufs=1))
+        stage_pool = ctx.enter_context(tc.tile_pool(name="stage", bufs=STAGE_BUFS))
+        psum_pool = ctx.enter_context(tc.psum_pool(name="acc", bufs=1))
+
+        x_raw = {}
+        x_grouped = {}
+        x_codes = {}
+        x_scales = {}
+        g_raw = {}
+        g_grouped = {}
+        g_codes = {}
+        g_scales = {}
+        acc = {}
+        stage = {}
+
+        def load_g(c):
+            g_raw[c] = graw_pool.tile([P, EXPERTS, PACK, RANK], BF16, name="g_raw%d" % c, tag="g_raw")
+            nc.sync.dma_start(
+                out=g_raw[c][:].rearrange("p e j r -> p e (j r)"),
+                in_=g_rows[:, c * K_PASS : (c + 1) * K_PASS, :].rearrange("e (p j) r -> p e (j r)", j=PACK),
+            )
+
+        def load_x(k):
+            h, c = divmod(k, PASSES)
+            x_raw[k] = raw_pool.tile([P, PACK, CHUNK], BF16, name="x_raw%d" % k, tag="x_raw")
+            nc.sync.dma_start(
+                out=x_raw[k][:],
+                in_=x_rows[c * K_PASS : (c + 1) * K_PASS, h * CHUNK : (h + 1) * CHUNK].rearrange(
+                    "(p j) w -> p j w", j=PACK
+                ),
+            )
+
+        def regroup_g(c):
+            g_grouped[c] = ggrouped_pool.tile(
+                [P, EXPERTS, RANK, PACK], BF16, name="g_grouped%d" % c, tag="g_grouped", align_bytes=64
+            )
+            nc.vector.tensor_copy(
+                out=g_grouped[c][:, 0:V_EXPERTS],
+                in_=g_raw[c][:, 0:V_EXPERTS].rearrange("p e j r -> p e r j"),
+            )
+            nc.scalar.copy(
+                out=g_grouped[c][:, V_EXPERTS:EXPERTS],
+                in_=g_raw[c][:, V_EXPERTS:EXPERTS].rearrange("p e j r -> p e r j"),
+            )
+
+        def regroup_x(k):
+            x_grouped[k] = grouped_pool.tile(
+                [P, CHUNK, PACK], BF16, name="x_grouped%d" % k, tag="x_grouped", align_bytes=64
+            )
+            nc.vector.tensor_copy(
+                out=x_grouped[k][:, 0:V_COLS, :].rearrange("p (c i) t -> p c t i", i=4),
+                in_=x_raw[k][:, :, 0:V_COLS].rearrange("p t (c i) -> p c t i", i=4),
+            )
+            nc.scalar.copy(
+                out=x_grouped[k][:, V_COLS:CHUNK, :].rearrange("p (c i) t -> p c t i", i=4),
+                in_=x_raw[k][:, :, V_COLS:CHUNK].rearrange("p t (c i) -> p c t i", i=4),
+            )
+
+        def quant_g(c):
+            g_codes[c] = keep_pool.tile([P, M_ALL], U32, name="g_codes%d" % c, align_bytes=64)
+            g_scales[c] = keep_pool.tile([P, M_ALL], U8, name="g_scales%d" % c, align_bytes=64)
+            nc.vector.quantize_mx(
+                out=g_codes[c][:].bitcast(E5M2X4),
+                scales=g_scales[c][:],
+                in_=g_grouped[c][:].rearrange("p e r j -> p (e r j)"),
+            )
+
+        def quant_x(k):
+            x_codes[k] = code_pool.tile([P, CHUNK], U32, name="x_codes%d" % k, tag="x_codes", align_bytes=64)
+            x_scales[k] = code_pool.tile([P, CHUNK], U8, name="x_scales%d" % k, tag="x_scales", align_bytes=64)
+            nc.vector.quantize_mx(
+                out=x_codes[k][:].bitcast(E4M3X4),
+                scales=x_scales[k][:],
+                in_=x_grouped[k][:].rearrange("p w j -> p (w j)"),
+            )
+
+        def pe_step(s):
+            for c in (3, 2, 1, 0):
+                m = (s - c) % M_TILES
+                k = s - m
+                if k < 0 or k >= CHUNKS:
+                    continue
+                m_cols = slice(m * P, (m + 1) * P)
+                for n in range(N_PER_CHUNK):
+                    n_cols = slice(n * N_TILE, (n + 1) * N_TILE)
+                    if c == 0:
+                        acc[(m, n)] = psum_pool.tile(
+                            [P, N_TILE], F32, name="acc%d_%d_%d" % (m, n, k), tag="bank%d_%d" % (m, n)
+                        )
+                    nc.tensor.matmul_mx(
+                        out=acc[(m, n)][:],
+                        lhsT=g_codes[c][:, m_cols].bitcast(E5M2X4),
+                        lhsT_scale=g_scales[c][:, m_cols],
+                        rhs=x_codes[k][:, n_cols].bitcast(E4M3X4),
+                        rhs_scale=x_scales[k][:, n_cols],
+                        start=(c == 0),
+                        stop=(c == PASSES - 1),
+                    )
+
+        def evacuate(j):
+            m = j % M_TILES
+            stage[j] = stage_pool.tile([P, CHUNK], F32, name="stage%d" % j, tag="stage")
+            for n in range(N_PER_CHUNK):
+                n_cols = slice(n * N_TILE, (n + 1) * N_TILE)
+                if n == 1 and j >= CHUNKS - TAIL_PAIRS:
+                    nc.vector.tensor_copy(out=stage[j][:, n_cols], in_=acc[(m, n)][:])
+                else:
+                    nc.scalar.copy(out=stage[j][:, n_cols], in_=acc[(m, n)][:])
+
+        def store(j):
+            h, m = divmod(j, M_TILES)
+            nc.sync.dma_start(
+                out=out_rows[m * P : (m + 1) * P, h * CHUNK : (h + 1) * CHUNK],
+                in_=stage[j][:],
+            )
+
+        for c in range(PASSES):
+            load_g(c)
+            load_x(c)
+        for k in range(PASSES, RAW_BUFS):
+            load_x(k)
+        regroup_g(0)
+        regroup_x(0)
+        last_load_step = CHUNKS - 1 - RAW_BUFS
+        for s in range(CHUNKS + M_TILES):
+            if s + 1 < PASSES:
+                regroup_g(s + 1)
+            if s + 1 < CHUNKS:
+                regroup_x(s + 1)
+            if s + RAW_BUFS < CHUNKS:
+                load_x(s + RAW_BUFS)
+            if s >= M_TILES:
+                evacuate(s - M_TILES)
+            for j in range(CHUNKS):
+                if max(j + M_TILES, last_load_step) == s:
+                    store(j)
+            if s < PASSES:
+                quant_g(s)
+            if s < CHUNKS:
+                quant_x(s)
+            if s < CHUNKS + M_TILES - 1:
+                pe_step(s)

@@ -67,10 +67,13 @@ def tile_moelineara_kernel(tc, x, W, grad_out, out):
 
         def load_g(c):
             g_raw[c] = graw_pool.tile([P, EXPERTS, PACK, RANK], BF16, name="g_raw%d" % c, tag="g_raw")
-            nc.sync.dma_start(
-                out=g_raw[c][:].rearrange("p e j r -> p e (j r)"),
-                in_=g_rows[:, c * K_PASS : (c + 1) * K_PASS, :].rearrange("e (p j) r -> p e (j r)", j=PACK),
-            )
+            for e0 in range(0, EXPERTS, 4):
+                nc.sync.dma_start(
+                    out=g_raw[c][:, e0 : e0 + 4].rearrange("p e j r -> p e (j r)"),
+                    in_=g_rows[e0 : e0 + 4, c * K_PASS : (c + 1) * K_PASS, :].rearrange(
+                        "e (p j) r -> p e (j r)", j=PACK
+                    ),
+                )
 
         def load_x(k):
             h, c = divmod(k, PASSES)

@@ -30,11 +30,11 @@ BYTES = TOKENS * D * 2 + TOKENS * M_ALL * 2 + M_ALL * D * 4
 
 RAW_BUFS = 10
 STAGE_BUFS = 12
-CODE_BUFS = 6
-GROUPED_BUFS = 3
+CODE_BUFS = 4
+GROUPED_BUFS = 4
 V_COLS = 672
 V_EXPERTS = 2
-TAIL_PAIRS = 4
+S_AHEAD = 2
 
 
 def tile_moelineara_kernel(tc, x, W, grad_out, out):
@@ -48,7 +48,7 @@ def tile_moelineara_kernel(tc, x, W, grad_out, out):
         raw_pool = ctx.enter_context(tc.tile_pool(name="raw", bufs=RAW_BUFS))
         graw_pool = ctx.enter_context(tc.tile_pool(name="graw", bufs=PASSES))
         grouped_pool = ctx.enter_context(tc.tile_pool(name="grouped", bufs=GROUPED_BUFS))
-        ggrouped_pool = ctx.enter_context(tc.tile_pool(name="ggrouped", bufs=2))
+        ggrouped_pool = ctx.enter_context(tc.tile_pool(name="ggrouped", bufs=S_AHEAD + 1))
         code_pool = ctx.enter_context(tc.tile_pool(name="codes", bufs=CODE_BUFS))
         keep_pool = ctx.enter_context(tc.tile_pool(name="keep", bufs=1))
         stage_pool = ctx.enter_context(tc.tile_pool(name="stage", bufs=STAGE_BUFS))
@@ -67,13 +67,10 @@ def tile_moelineara_kernel(tc, x, W, grad_out, out):
 
         def load_g(c):
             g_raw[c] = graw_pool.tile([P, EXPERTS, PACK, RANK], BF16, name="g_raw%d" % c, tag="g_raw")
-            for e0 in range(0, EXPERTS, 4):
-                nc.sync.dma_start(
-                    out=g_raw[c][:, e0 : e0 + 4].rearrange("p e j r -> p e (j r)"),
-                    in_=g_rows[e0 : e0 + 4, c * K_PASS : (c + 1) * K_PASS, :].rearrange(
-                        "e (p j) r -> p e (j r)", j=PACK
-                    ),
-                )
+            nc.sync.dma_start(
+                out=g_raw[c][:].rearrange("p e j r -> p e (j r)"),
+                in_=g_rows[:, c * K_PASS : (c + 1) * K_PASS, :].rearrange("e (p j) r -> p e (j r)", j=PACK),
+            )
 
         def load_x(k):
             h, c = divmod(k, PASSES)
@@ -85,31 +82,47 @@ def tile_moelineara_kernel(tc, x, W, grad_out, out):
                 ),
             )
 
-        def regroup_g(c):
+        def regroup_g_scalar(c):
             g_grouped[c] = ggrouped_pool.tile(
                 [P, EXPERTS, RANK, PACK], BF16, name="g_grouped%d" % c, tag="g_grouped", align_bytes=64
-            )
-            nc.vector.tensor_copy(
-                out=g_grouped[c][:, 0:V_EXPERTS],
-                in_=g_raw[c][:, 0:V_EXPERTS].rearrange("p e j r -> p e r j"),
             )
             nc.scalar.copy(
                 out=g_grouped[c][:, V_EXPERTS:EXPERTS],
                 in_=g_raw[c][:, V_EXPERTS:EXPERTS].rearrange("p e j r -> p e r j"),
             )
 
-        def regroup_x(k):
+        def regroup_g_vector(c):
+            nc.vector.tensor_copy(
+                out=g_grouped[c][:, 0:V_EXPERTS],
+                in_=g_raw[c][:, 0:V_EXPERTS].rearrange("p e j r -> p e r j"),
+            )
+
+        def regroup_x_scalar(k):
             x_grouped[k] = grouped_pool.tile(
                 [P, CHUNK, PACK], BF16, name="x_grouped%d" % k, tag="x_grouped", align_bytes=64
-            )
-            nc.vector.tensor_copy(
-                out=x_grouped[k][:, 0:V_COLS, :].rearrange("p (c i) t -> p c t i", i=4),
-                in_=x_raw[k][:, :, 0:V_COLS].rearrange("p t (c i) -> p c t i", i=4),
             )
             nc.scalar.copy(
                 out=x_grouped[k][:, V_COLS:CHUNK, :].rearrange("p (c i) t -> p c t i", i=4),
                 in_=x_raw[k][:, :, V_COLS:CHUNK].rearrange("p t (c i) -> p c t i", i=4),
             )
+
+        def regroup_x_vector(k):
+            nc.vector.tensor_copy(
+                out=x_grouped[k][:, 0:V_COLS, :].rearrange("p (c i) t -> p c t i", i=4),
+                in_=x_raw[k][:, :, 0:V_COLS].rearrange("p t (c i) -> p c t i", i=4),
+            )
+
+        def scalar_regroups(k):
+            if k < PASSES:
+                regroup_g_scalar(k)
+            if k < CHUNKS:
+                regroup_x_scalar(k)
+
+        def vector_regroups(k):
+            if k < PASSES:
+                regroup_g_vector(k)
+            if k < CHUNKS:
+                regroup_x_vector(k)
 
         def quant_g(c):
             g_codes[c] = keep_pool.tile([P, M_ALL], U32, name="g_codes%d" % c, align_bytes=64)
@@ -129,12 +142,9 @@ def tile_moelineara_kernel(tc, x, W, grad_out, out):
                 in_=x_grouped[k][:].rearrange("p w j -> p (w j)"),
             )
 
-        def pe_step(s):
-            for c in (3, 2, 1, 0):
-                m = (s - c) % M_TILES
-                k = s - m
-                if k < 0 or k >= CHUNKS:
-                    continue
+        def pe_step(k):
+            c = k % PASSES
+            for m in range(M_TILES):
                 m_cols = slice(m * P, (m + 1) * P)
                 for n in range(N_PER_CHUNK):
                     n_cols = slice(n * N_TILE, (n + 1) * N_TILE)
@@ -152,46 +162,46 @@ def tile_moelineara_kernel(tc, x, W, grad_out, out):
                         stop=(c == PASSES - 1),
                     )
 
-        def evacuate(j):
-            m = j % M_TILES
-            stage[j] = stage_pool.tile([P, CHUNK], F32, name="stage%d" % j, tag="stage")
-            for n in range(N_PER_CHUNK):
-                n_cols = slice(n * N_TILE, (n + 1) * N_TILE)
-                if n == 1 and j >= CHUNKS - TAIL_PAIRS:
-                    nc.vector.tensor_copy(out=stage[j][:, n_cols], in_=acc[(m, n)][:])
-                else:
-                    nc.scalar.copy(out=stage[j][:, n_cols], in_=acc[(m, n)][:])
+        def evacuate(h, vector_helps):
+            for m in range(M_TILES):
+                j = h * M_TILES + m
+                stage[j] = stage_pool.tile([P, CHUNK], F32, name="stage%d" % j, tag="stage")
+                for n in range(N_PER_CHUNK):
+                    n_cols = slice(n * N_TILE, (n + 1) * N_TILE)
+                    if n == 1 and vector_helps:
+                        nc.vector.tensor_copy(out=stage[j][:, n_cols], in_=acc[(m, n)][:])
+                    else:
+                        nc.scalar.copy(out=stage[j][:, n_cols], in_=acc[(m, n)][:])
 
-        def store(j):
-            h, m = divmod(j, M_TILES)
-            nc.sync.dma_start(
-                out=out_rows[m * P : (m + 1) * P, h * CHUNK : (h + 1) * CHUNK],
-                in_=stage[j][:],
-            )
+        def store(h):
+            for m in range(M_TILES):
+                nc.sync.dma_start(
+                    out=out_rows[m * P : (m + 1) * P, h * CHUNK : (h + 1) * CHUNK],
+                    in_=stage[h * M_TILES + m][:],
+                )
 
         for c in range(PASSES):
             load_g(c)
             load_x(c)
         for k in range(PASSES, RAW_BUFS):
             load_x(k)
-        regroup_g(0)
-        regroup_x(0)
+        for k in range(S_AHEAD):
+            scalar_regroups(k)
+        vector_regroups(0)
         last_load_step = CHUNKS - 1 - RAW_BUFS
-        for s in range(CHUNKS + M_TILES):
-            if s + 1 < PASSES:
-                regroup_g(s + 1)
-            if s + 1 < CHUNKS:
-                regroup_x(s + 1)
+        for s in range(CHUNKS):
+            if s % PASSES == 0 and s > 0:
+                evacuate(s // PASSES - 1, False)
+            scalar_regroups(s + S_AHEAD)
+            vector_regroups(s + 1)
             if s + RAW_BUFS < CHUNKS:
                 load_x(s + RAW_BUFS)
-            if s >= M_TILES:
-                evacuate(s - M_TILES)
-            for j in range(CHUNKS):
-                if max(j + M_TILES, last_load_step) == s:
-                    store(j)
+            for h in range(ROUNDS - 1):
+                if max((h + 1) * PASSES, last_load_step) == s:
+                    store(h)
             if s < PASSES:
                 quant_g(s)
-            if s < CHUNKS:
-                quant_x(s)
-            if s < CHUNKS + M_TILES - 1:
-                pe_step(s)
+            quant_x(s)
+            pe_step(s)
+        evacuate(ROUNDS - 1, True)
+        store(ROUNDS - 1)

from contextlib import ExitStack

import concourse.mybir as mybir

BF16 = mybir.dt.bfloat16
F32 = mybir.dt.float32
U32 = mybir.dt.uint32
U8 = mybir.dt.uint8
E4M3X4 = mybir.dt.float8_e4m3fn_x4
E5M2X4 = mybir.dt.float8_e5m2_x4

P = 128
PACK = 4
K_PASS = P * PACK
TOKENS = 2048
D = 4096
EXPERTS = 8
RANK = 64
M_ALL = EXPERTS * RANK
PASSES = TOKENS // K_PASS
M_TILES = M_ALL // P
N_TILE = 512
CHUNK = 1024
N_PER_CHUNK = CHUNK // N_TILE
ROUNDS = D // CHUNK
CHUNKS = ROUNDS * PASSES

FLOPS = 2 * TOKENS * M_ALL * D
BYTES = TOKENS * D * 2 + TOKENS * M_ALL * 2 + M_ALL * D * 4

RAW_BUFS = 10
STAGE_BUFS = 12
CODE_BUFS = 4
GROUPED_BUFS = 4
V_COLS = 672
V_EXPERTS = 2
S_AHEAD = 2


def tile_moelineara_kernel(tc, x, W, grad_out, out):
    nc = tc.nc
    x_rows = x.rearrange("b s d -> (b s) d")
    g_rows = grad_out.rearrange("e b s r -> e (b s) r")
    out_rows = out.rearrange("e r d -> (e r) d")

    with ExitStack() as ctx:
        ctx.enter_context(tc.manual_schedule())
        raw_pool = ctx.enter_context(tc.tile_pool(name="raw", bufs=RAW_BUFS))
        graw_pool = ctx.enter_context(tc.tile_pool(name="graw", bufs=PASSES))
        grouped_pool = ctx.enter_context(tc.tile_pool(name="grouped", bufs=GROUPED_BUFS))
        ggrouped_pool = ctx.enter_context(tc.tile_pool(name="ggrouped", bufs=S_AHEAD + 1))
        code_pool = ctx.enter_context(tc.tile_pool(name="codes", bufs=CODE_BUFS))
        keep_pool = ctx.enter_context(tc.tile_pool(name="keep", bufs=1))
        stage_pool = ctx.enter_context(tc.tile_pool(name="stage", bufs=STAGE_BUFS))
        psum_pool = ctx.enter_context(tc.psum_pool(name="acc", bufs=1))

        x_raw = {}
        x_grouped = {}
        x_codes = {}
        x_scales = {}
        g_raw = {}
        g_grouped = {}
        g_codes = {}
        g_scales = {}
        acc = {}
        stage = {}

        def load_g(c):
            g_raw[c] = graw_pool.tile([P, EXPERTS, PACK, RANK], BF16, name="g_raw%d" % c, tag="g_raw")
            nc.sync.dma_start(
                out=g_raw[c][:].rearrange("p e j r -> p e (j r)"),
                in_=g_rows[:, c * K_PASS : (c + 1) * K_PASS, :].rearrange("e (p j) r -> p e (j r)", j=PACK),
            )

        def load_x(k):
            h, c = divmod(k, PASSES)
            x_raw[k] = raw_pool.tile([P, PACK, CHUNK], BF16, name="x_raw%d" % k, tag="x_raw")
            nc.sync.dma_start(
                out=x_raw[k][:],
                in_=x_rows[c * K_PASS : (c + 1) * K_PASS, h * CHUNK : (h + 1) * CHUNK].rearrange(
                    "(p j) w -> p j w", j=PACK
                ),
            )

        def regroup_g_scalar(c):
            g_grouped[c] = ggrouped_pool.tile(
                [P, EXPERTS, RANK, PACK], BF16, name="g_grouped%d" % c, tag="g_grouped", align_bytes=64
            )
            nc.scalar.copy(
                out=g_grouped[c][:, V_EXPERTS:EXPERTS],
                in_=g_raw[c][:, V_EXPERTS:EXPERTS].rearrange("p e j r -> p e r j"),
            )

        def regroup_g_vector(c):
            nc.vector.tensor_copy(
                out=g_grouped[c][:, 0:V_EXPERTS],
                in_=g_raw[c][:, 0:V_EXPERTS].rearrange("p e j r -> p e r j"),
            )

        def regroup_x_scalar(k):
            x_grouped[k] = grouped_pool.tile(
                [P, CHUNK, PACK], BF16, name="x_grouped%d" % k, tag="x_grouped", align_bytes=64
            )
            nc.scalar.copy(
                out=x_grouped[k][:, V_COLS:CHUNK, :].rearrange("p (c i) t -> p c t i", i=4),
                in_=x_raw[k][:, :, V_COLS:CHUNK].rearrange("p t (c i) -> p c t i", i=4),
            )

        def regroup_x_vector(k):
            nc.vector.tensor_copy(
                out=x_grouped[k][:, 0:V_COLS, :].rearrange("p (c i) t -> p c t i", i=4),
                in_=x_raw[k][:, :, 0:V_COLS].rearrange("p t (c i) -> p c t i", i=4),
            )

        def scalar_regroups(k):
            if k < PASSES:
                regroup_g_scalar(k)
            if k < CHUNKS:
                regroup_x_scalar(k)

        def vector_regroups(k):
            if k < PASSES:
                regroup_g_vector(k)
            if k < CHUNKS:
                regroup_x_vector(k)

        def quant_g(c):
            g_codes[c] = keep_pool.tile([P, M_ALL], U32, name="g_codes%d" % c, align_bytes=64)
            g_scales[c] = keep_pool.tile([P, M_ALL], U8, name="g_scales%d" % c, align_bytes=64)
            nc.vector.quantize_mx(
                out=g_codes[c][:].bitcast(E5M2X4),
                scales=g_scales[c][:],
                in_=g_grouped[c][:].rearrange("p e r j -> p (e r j)"),
            )

        def quant_x(k):
            x_codes[k] = code_pool.tile([P, CHUNK], U32, name="x_codes%d" % k, tag="x_codes", align_bytes=64)
            x_scales[k] = code_pool.tile([P, CHUNK], U8, name="x_scales%d" % k, tag="x_scales", align_bytes=64)
            nc.vector.quantize_mx(
                out=x_codes[k][:].bitcast(E4M3X4),
                scales=x_scales[k][:],
                in_=x_grouped[k][:].rearrange("p w j -> p (w j)"),
            )

        def pe_step(k):
            c = k % PASSES
            for m in range(M_TILES):
                m_cols = slice(m * P, (m + 1) * P)
                for n in range(N_PER_CHUNK):
                    n_cols = slice(n * N_TILE, (n + 1) * N_TILE)
                    if c == 0:
                        acc[(m, n)] = psum_pool.tile(
                            [P, N_TILE], F32, name="acc%d_%d_%d" % (m, n, k), tag="bank%d_%d" % (m, n)
                        )
                    nc.tensor.matmul_mx(
                        out=acc[(m, n)][:],
                        lhsT=g_codes[c][:, m_cols].bitcast(E5M2X4),
                        lhsT_scale=g_scales[c][:, m_cols],
                        rhs=x_codes[k][:, n_cols].bitcast(E4M3X4),
                        rhs_scale=x_scales[k][:, n_cols],
                        start=(c == 0),
                        stop=(c == PASSES - 1),
                    )

        def evacuate(h, vector_helps):
            for m in range(M_TILES):
                j = h * M_TILES + m
                stage[j] = stage_pool.tile([P, CHUNK], F32, name="stage%d" % j, tag="stage")
                for n in range(N_PER_CHUNK):
                    n_cols = slice(n * N_TILE, (n + 1) * N_TILE)
                    if n == 1 and vector_helps:
                        nc.vector.tensor_copy(out=stage[j][:, n_cols], in_=acc[(m, n)][:])
                    else:
                        nc.scalar.copy(out=stage[j][:, n_cols], in_=acc[(m, n)][:])

        def store(h):
            for m in range(M_TILES):
                nc.sync.dma_start(
                    out=out_rows[m * P : (m + 1) * P, h * CHUNK : (h + 1) * CHUNK],
                    in_=stage[h * M_TILES + m][:],
                )

        for c in range(PASSES):
            load_g(c)
            load_x(c)
        for k in range(PASSES, RAW_BUFS):
            load_x(k)
        for k in range(S_AHEAD):
            scalar_regroups(k)
        vector_regroups(0)
        last_load_step = CHUNKS - 1 - RAW_BUFS
        for s in range(CHUNKS):
            if s % PASSES == 0 and s > 0:
                evacuate(s // PASSES - 1, False)
            scalar_regroups(s + S_AHEAD)
            vector_regroups(s + 1)
            if s + RAW_BUFS < CHUNKS:
                load_x(s + RAW_BUFS)
            for h in range(ROUNDS - 1):
                if max((h + 1) * PASSES, last_load_step) == s:
                    store(h)
            if s < PASSES:
                quant_g(s)
            quant_x(s)
            pe_step(s)
        evacuate(ROUNDS - 1, True)
        store(ROUNDS - 1)
